import numpy as np
import ml_dtypes


def mxq(x, axis, fmt="e4m3"):
    dtype, down = {"e4m3": (ml_dtypes.float8_e4m3fn, 7), "e5m2": (ml_dtypes.float8_e5m2, 14)}[fmt]
    v = np.moveaxis(np.asarray(x, np.float32).astype(ml_dtypes.bfloat16).astype(np.float64), axis, -1)
    blocks = v.reshape(v.shape[:-1] + (-1, 32))
    amax = np.abs(blocks).max(-1, keepdims=True)
    byte = np.maximum(np.where(amax > 0, np.frexp(amax)[1] - 1 + 127, 0) - down, 1)
    scale = np.exp2(byte - 127.0)
    codes = (blocks / scale).astype(np.float32).astype(dtype).astype(np.float64)
    return np.moveaxis((codes * scale).reshape(v.shape), -1, axis)


WIDE = False


def mx_kscale(k):
    if not WIDE:
        return np.ones(k)
    levels = np.array([10, -10, 5, -5, 0])
    if k % 512:
        return np.exp2(np.random.permutation(np.resize(levels, k // 32))).repeat(32)
    a = np.empty((k // 512, 16))
    for p in range(k // 512):
        a[p, :8] = np.random.permutation(np.resize(levels, 8))
        for g in range(8):
            far = levels[np.abs(levels - a[p, g]) >= 10]
            a[p, g + 8] = far[np.random.randint(len(far))]
    return np.exp2(a.ravel()).repeat(32)


BF16 = ml_dtypes.bfloat16


def bf(x):
    return np.asarray(x, np.float32).astype(BF16)


def f64(x):
    return np.asarray(x).astype(np.float64)


N, E, G, M, H = 4096, 512, 512, 256, 1
HG = H * G


def sigmoid(v):
    return 1.0 / (1.0 + np.exp(-v))


def setup_inputs():
    r = np.random.standard_normal
    s = mx_kscale(E)
    t = np.tile(mx_kscale(G), H)
    return {"q": bf(r((N, E)) * s),
            "rep": bf(r((N, E)) * s),
            "Wq": bf(r((E, HG)) * G ** 0.25 / np.sqrt(E) / s[:, None]),
            "Wk": bf(r((E, HG)) * G ** 0.25 / np.sqrt(E) / s[:, None]),
            "Wv": bf(r((E, HG)) / np.sqrt(E) / s[:, None] * t),
            "W1": bf(r((H, G, M)) * 2.0 / np.sqrt(G) / t.reshape(H, G, 1)),
            "b1": bf(r((H, M)) * 0.2)}


def reference(q, rep, Wq, Wk, Wv, W1, b1):
    qq = mxq(f64(q), 1, "e4m3")
    rq = mxq(f64(rep), 1, "e4m3")
    Qh = (qq @ mxq(f64(Wq), 0, "e4m3")).reshape(N, H, G)
    Kh = (rq @ mxq(f64(Wk), 0, "e4m3")).reshape(N, H, G)
    Vh = (rq @ mxq(f64(Wv), 0, "e4m3")).reshape(N, H, G)
    gate = sigmoid(Qh * Kh * (1.0 / np.sqrt(G)))
    z = gate * Vh
    zt = z.transpose(1, 0, 2)
    pre = (mxq(zt, 2, "e4m3") @ mxq(f64(W1), 1, "e4m3")).transpose(1, 0, 2)
    return np.maximum(pre + f64(b1), 0.0)

@@ -1,0 +1,294 @@
+import math
+from contextlib import ExitStack
+
+import concourse.mybir as mybir
+from concourse.masks import make_identity
+
+F32 = mybir.dt.float32
+BF16 = mybir.dt.bfloat16
+U32 = mybir.dt.uint32
+U8 = mybir.dt.uint8
+FP8X4 = mybir.dt.float8_e4m3fn_x4
+ALU = mybir.AluOpType
+ACT = mybir.ActivationFunctionType
+
+P = 128
+NODES, E, G, M = 4096, 512, 512, 256
+TILES = NODES // P
+PAIRS = TILES // 2
+FLOPS = 2 * NODES * E * 3 * G + 2 * NODES * G * M
+
+CHUNKS = [(0, 2), (2, 4)] + [(j, j + 4) for j in range(4, TILES, 4)]
+
+
+def tile_treehopnode_pa_t_kernel(tc, q, rep, Wq, Wk, Wv, W1, b1, out):
+    nc = tc.nc
+    q_view = q.rearrange("(p j) e -> p j e", j=TILES)
+    rep_view = rep.rearrange("(p j) e -> p j e", j=TILES)
+    out_view = out.rearrange("(p j) h m -> p j (h m)", j=TILES)
+
+    with ExitStack() as ctx:
+        const = ctx.enter_context(tc.tile_pool(name="const", bufs=1))
+        grp_pool = ctx.enter_context(tc.tile_pool(name="grp_pool", bufs=3))
+        code_pool = ctx.enter_context(tc.tile_pool(name="code_pool", bufs=4))
+        f32_pool = ctx.enter_context(tc.tile_pool(name="f32_pool", bufs=3))
+        z_pool = ctx.enter_context(tc.tile_pool(name="z_pool", bufs=3))
+        o_pool = ctx.enter_context(tc.tile_pool(name="o_pool", bufs=4))
+        tb_pool = ctx.enter_context(tc.psum_pool(name="tb_pool", bufs=2))
+        qb_pool = ctx.enter_context(tc.psum_pool(name="qb_pool", bufs=2))
+        kb_pool = ctx.enter_context(tc.psum_pool(name="kb_pool", bufs=2))
+        vb_pool = ctx.enter_context(tc.psum_pool(name="vb_pool", bufs=1))
+        ob_pool = ctx.enter_context(tc.psum_pool(name="ob_pool", bufs=1))
+        ctx.enter_context(tc.manual_schedule())
+
+        bias = const.tile([P, M], BF16, name="bias")
+
+        w_raw = {}
+        for key, w in (("q", Wq), ("k", Wk), ("v", Wv)):
+            w_raw[key] = const.tile([P, 4 * G], BF16, name="w_raw_" + key)
+            nc.sync.dma_start(
+                out=w_raw[key][:],
+                in_=w.rearrange("(p j) g -> p (j g)", j=4),
+            )
+        w1_raw = const.tile([P, 4 * M], BF16, name="w1_raw")
+        x_raw = {}
+        where = {}
+        for c, (j0, j1) in enumerate(CHUNKS):
+            for a, view in enumerate((q_view, rep_view)):
+                x_raw[(a, c)] = const.tile([P, (j1 - j0) * E], BF16, name="x_raw_%d_%d" % (a, c))
+                nc.sync.dma_start(
+                    out=x_raw[(a, c)][:].rearrange("p (j e) -> p j e", e=E),
+                    in_=view[:, j0:j1, :],
+                )
+            for j in range(j0, j1):
+                where[j] = (c, j - j0)
+            if c == 0:
+                nc.sync.dma_start(out=w1_raw[:], in_=W1.rearrange("h (p j) m -> (h p) (j m)", j=4))
+            if c == 2:
+                nc.sync.dma_start(
+                    out=bias[:], in_=b1.rearrange("h m -> (h m)").partition_broadcast(P)
+                )
+
+        ident = const.tile([P, P], F32, name="ident")
+        make_identity(nc, ident[:])
+        warm_in = const.tile([P, 1], F32, name="warm_in")
+        warm_out = const.tile([P, 1], F32, name="warm_out")
+        nc.vector.memset(warm_in[:], 0.0)
+        nc.scalar.activation(out=warm_out[:], in_=warm_in[:], func=ACT.Sigmoid)
+
+        w_grp = {}
+        w_code = {}
+        w_scale = {}
+        for key in ("q", "k", "v"):
+            w_grp[key] = const.tile([P, 4 * G], BF16, name="w_grp_" + key, align_bytes=64)
+            w_code[key] = const.tile([P, G], U32, name="w_code_" + key, align_bytes=64)
+            w_scale[key] = const.tile([P, G], U8, name="w_scale_" + key, align_bytes=64)
+        w1_grp = const.tile([P, 4 * M], BF16, name="w1_grp", align_bytes=64)
+        w1_code = const.tile([P, M], U32, name="w1_code", align_bytes=64)
+        w1_scale = const.tile([P, M], U8, name="w1_scale", align_bytes=64)
+
+        def regroup_w(key):
+            src = w_raw[key][:].rearrange("p (j c t) -> p t c j", j=4, t=4)
+            dst = w_grp[key][:].rearrange("p (t c j) -> p t c j", t=4, j=4)
+            nc.vector.tensor_copy(out=dst[:, 0:2], in_=src[:, 0:2])
+            nc.scalar.copy(out=dst[:, 2:4], in_=src[:, 2:4])
+
+        def quantise_w(key):
+            nc.vector.quantize_mx(
+                out=w_code[key][:].bitcast(FP8X4), scales=w_scale[key][:], in_=w_grp[key][:]
+            )
+
+        regroup_w("q")
+        regroup_w("k")
+        quantise_w("q")
+        regroup_w("v")
+        quantise_w("k")
+        quantise_w("v")
+
+        tb = {}
+        grp = {}
+        x_code = {}
+        x_scale = {}
+        banks = {}
+        q_sb = {}
+        prod = {}
+        gate = {}
+        z_grp = {}
+        z_code = {}
+        z_scale = {}
+        o_bank = {}
+        o_sb = {}
+
+        def transposes(r):
+            for j in (2 * r, 2 * r + 1):
+                c, jj = where[j]
+                tb[j] = tb_pool.tile([P, 512], F32, name="tb")
+                for a in range(2):
+                    words = x_raw[(a, c)][:].bitcast(F32)
+                    for u in range(2):
+                        s = 2 * a + u
+                        w0 = jj * (E // 2) + u
+                        nc.tensor.transpose(
+                            out=tb[j][:, s * P : (s + 1) * P],
+                            in_=words[:, w0 : w0 + 2 * P - 1 : 2],
+                            identity=ident[:],
+                        )
+
+        def evacuate(j):
+            r, i = divmod(j, 2)
+            if i == 0:
+                grp[r] = grp_pool.tile([P, 2048], BF16, name="grp", align_bytes=64)
+            nc.scalar.copy(
+                out=grp[r][:, i * 1024 : (i + 1) * 1024]
+                .bitcast(F32)
+                .rearrange("p (a n u) -> p a n u", a=2, u=2),
+                in_=tb[j][:].rearrange("p (a u n) -> p a n u", a=2, u=2),
+            )
+
+        def quantise_x(r):
+            x_code[r] = code_pool.tile([P, 512], U32, name="x_code", align_bytes=64)
+            x_scale[r] = code_pool.tile([P, 512], U8, name="x_scale", align_bytes=64)
+            nc.vector.quantize_mx(
+                out=x_code[r][:].bitcast(FP8X4), scales=x_scale[r][:], in_=grp[r][:]
+            )
+
+        def project(key, j):
+            r, i = divmod(j, 2)
+            a = 0 if key == "q" else 1
+            pool = {"q": qb_pool, "k": kb_pool, "v": vb_pool}[key]
+            bank = pool.tile([P, 512], F32, name="bank_" + key)
+            banks[(key, j)] = bank
+            c0 = (2 * i + a) * P
+            for t in range(4):
+                nc.tensor.matmul_mx(
+                    out=bank[:, t * P : (t + 1) * P],
+                    lhsT=w_code[key][:, t * P : (t + 1) * P].bitcast(FP8X4),
+                    lhsT_scale=w_scale[key][:, t * P : (t + 1) * P],
+                    rhs=x_code[r][:, c0 : c0 + P].bitcast(FP8X4),
+                    rhs_scale=x_scale[r][:, c0 : c0 + P],
+                    start=True,
+                    stop=True,
+                )
+
+        def by_node(ap):
+            return ap
+
+        def flat(ap):
+            return ap
+
+        def copy_q(j):
+            q_sb[j] = f32_pool.tile([P, 512], F32, name="q_sb")
+            nc.scalar.copy(out=flat(q_sb[j][:]), in_=by_node(banks[("q", j)][:]))
+
+        def product(j):
+            prod[j] = f32_pool.tile([P, 512], F32, name="prod")
+            nc.vector.tensor_tensor(
+                out=flat(prod[j][:]), in0=flat(q_sb[j][:]), in1=by_node(banks[("k", j)][:]), op=ALU.mult
+            )
+
+        def sigmoid(j):
+            gate[j] = f32_pool.tile([P, 512], F32, name="gate")
+            nc.scalar.activation(
+                out=gate[j][:], in_=prod[j][:], func=ACT.Sigmoid, scale=1.0 / math.sqrt(G)
+            )
+
+        def gated(j):
+            r, i = divmod(j, 2)
+            if i == 0:
+                z_grp[r] = z_pool.tile([P, 1024], BF16, name="z_grp", align_bytes=64)
+            nc.vector.tensor_tensor(
+                out=z_grp[r][:, i * 512 : (i + 1) * 512].rearrange("p (c i t) -> p c t i", i=4, t=4),
+                in0=gate[j][:].rearrange("p (t c i) -> p c t i", t=4, i=4),
+                in1=banks[("v", j)][:].rearrange("p (t c i) -> p c t i", t=4, i=4),
+                op=ALU.mult,
+            )
+
+        def quantise_z(r):
+            z_code[r] = z_pool.tile([P, 256], U32, name="z_code", align_bytes=64)
+            z_scale[r] = z_pool.tile([P, 256], U8, name="z_scale", align_bytes=64)
+            nc.vector.quantize_mx(
+                out=z_code[r][:].bitcast(FP8X4), scales=z_scale[r][:], in_=z_grp[r][:]
+            )
+
+        def layer(r):
+            o_bank[r] = ob_pool.tile([P, 512], F32, name="o_bank")
+            for i in range(2):
+                nc.tensor.matmul_mx(
+                    out=o_bank[r][:, i * M : (i + 1) * M],
+                    lhsT=z_code[r][:, i * P : (i + 1) * P].bitcast(FP8X4),
+                    lhsT_scale=z_scale[r][:, i * P : (i + 1) * P],
+                    rhs=w1_code[:].bitcast(FP8X4),
+                    rhs_scale=w1_scale[:],
+                    start=True,
+                    stop=True,
+                )
+
+        def finish(r):
+            o_sb[r] = o_pool.tile([P, 512], F32, name="o_sb")
+            nc.vector.tensor_tensor(
+                out=o_sb[r][:].rearrange("p (i m) -> p i m", i=2),
+                in0=o_bank[r][:].rearrange("p (i m) -> p i m", i=2),
+                in1=bias[:].unsqueeze(1).to_broadcast([P, 2, M]),
+                op=ALU.add,
+            )
+
+        def relu_store(r):
+            nc.scalar.activation(out=o_sb[r][:], in_=o_sb[r][:], func=ACT.Relu)
+            nc.sync.dma_start(
+                out=out_view[:, 2 * r : 2 * r + 2, :],
+                in_=o_sb[r][:].rearrange("p (j m) -> p j m", m=M),
+            )
+
+        def ok(r):
+            return 0 <= r < PAIRS
+
+        for r in range(-3, PAIRS + 2):
+            if ok(r - 2):
+                layer(r - 2)
+            if ok(r):
+                copy_q(2 * r + 1)
+                product(2 * r)
+                sigmoid(2 * r)
+            if ok(r - 1):
+                gated(2 * r - 1)
+            if ok(r):
+                project("k", 2 * r + 1)
+            if ok(r + 1):
+                project("q", 2 * r + 2)
+            if ok(r - 2):
+                finish(r - 2)
+            if ok(r):
+                project("v", 2 * r)
+            if ok(r + 2):
+                evacuate(2 * r + 4)
+                evacuate(2 * r + 5)
+            if ok(r + 1):
+                project("q", 2 * r + 3)
+            if ok(r):
+                product(2 * r + 1)
+                sigmoid(2 * r + 1)
+            if ok(r + 1):
+                project("k", 2 * r + 2)
+            if ok(r):
+                gated(2 * r)
+            if ok(r + 3):
+                transposes(r + 3)
+            if ok(r):
+                project("v", 2 * r + 1)
+            if ok(r + 1):
+                copy_q(2 * r + 2)
+            if ok(r - 2):
+                relu_store(r - 2)
+            if ok(r - 1):
+                quantise_z(r - 1)
+            if ok(r + 2):
+                quantise_x(r + 2)
+            if r == -2:
+                nc.vector.tensor_copy(
+                    out=w1_grp[:].rearrange("p (m j) -> p m j", j=4),
+                    in_=w1_raw[:].rearrange("p (j m) -> p m j", j=4),
+                )
+            if r == -1:
+                nc.vector.quantize_mx(
+                    out=w1_code[:].bitcast(FP8X4), scales=w1_scale[:], in_=w1_grp[:]
+                )

@@ -88,10 +88,10 @@ def tile_treehopnode_pa_t_kernel(tc, q, rep, Wq, Wk, Wv, W1, b1, out):
         w1_scale = const.tile([P, M], U8, name="w1_scale", align_bytes=64)
 
         def regroup_w(key):
-            src = w_raw[key][:].rearrange("p (j c t) -> p t c j", j=4, t=4)
-            dst = w_grp[key][:].rearrange("p (t c j) -> p t c j", t=4, j=4)
-            nc.vector.tensor_copy(out=dst[:, 0:2], in_=src[:, 0:2])
-            nc.scalar.copy(out=dst[:, 2:4], in_=src[:, 2:4])
+            src = w_raw[key][:].rearrange("p (j c t) -> p c j t", j=4, t=4)
+            dst = w_grp[key][:].rearrange("p (t c j) -> p c j t", t=4, j=4)
+            nc.vector.tensor_copy(out=dst[:, 0:64], in_=src[:, 0:64])
+            nc.scalar.copy(out=dst[:, 64:128], in_=src[:, 64:128])
 
         def quantise_w(key):
             nc.vector.quantize_mx(

@@ -197,9 +197,9 @@ def tile_treehopnode_pa_t_kernel(tc, q, rep, Wq, Wk, Wv, W1, b1, out):
             if i == 0:
                 z_grp[r] = z_pool.tile([P, 1024], BF16, name="z_grp", align_bytes=64)
             nc.vector.tensor_tensor(
-                out=z_grp[r][:, i * 512 : (i + 1) * 512].rearrange("p (c i t) -> p c t i", i=4, t=4),
-                in0=gate[j][:].rearrange("p (t c i) -> p c t i", t=4, i=4),
-                in1=banks[("v", j)][:].rearrange("p (t c i) -> p c t i", t=4, i=4),
+                out=z_grp[r][:, i * 512 : (i + 1) * 512].rearrange("p (c i t) -> p c t i", i=2, t=4),
+                in0=gate[j][:].rearrange("p (t c i) -> p c t i", t=4, i=2),
+                in1=banks[("v", j)][:].rearrange("p (t c i) -> p c t i", t=4, i=2),
                 op=ALU.mult,
             )
 

@@ -18,8 +18,6 @@ TILES = NODES // P
 PAIRS = TILES // 2
 FLOPS = 2 * NODES * E * 3 * G + 2 * NODES * G * M
 
-CHUNKS = [(0, 2), (2, 4)] + [(j, j + 4) for j in range(4, TILES, 4)]
-
 
 def tile_treehopnode_pa_t_kernel(tc, q, rep, Wq, Wk, Wv, W1, b1, out):
     nc = tc.nc
@@ -41,33 +39,35 @@ def tile_treehopnode_pa_t_kernel(tc, q, rep, Wq, Wk, Wv, W1, b1, out):
         ob_pool = ctx.enter_context(tc.psum_pool(name="ob_pool", bufs=1))
         ctx.enter_context(tc.manual_schedule())
 
-        bias = const.tile([P, M], BF16, name="bias")
-
         w_raw = {}
-        for key, w in (("q", Wq), ("k", Wk), ("v", Wv)):
-            w_raw[key] = const.tile([P, 4 * G], BF16, name="w_raw_" + key)
-            nc.sync.dma_start(
-                out=w_raw[key][:],
-                in_=w.rearrange("(p j) g -> p (j g)", j=4),
-            )
-        w1_raw = const.tile([P, 4 * M], BF16, name="w1_raw")
         x_raw = {}
-        where = {}
-        for c, (j0, j1) in enumerate(CHUNKS):
+
+        def load_w(key, w):
+            w_raw[key] = const.tile([P, 4 * G], BF16, name="w_raw_" + key)
+            nc.sync.dma_start(out=w_raw[key][:], in_=w.rearrange("(p j) g -> p (j g)", j=4))
+
+        def load_x(j0, j1):
             for a, view in enumerate((q_view, rep_view)):
-                x_raw[(a, c)] = const.tile([P, (j1 - j0) * E], BF16, name="x_raw_%d_%d" % (a, c))
+                chunk = const.tile([P, (j1 - j0) * E], BF16, name="x_raw_%d_%d" % (a, j0))
                 nc.sync.dma_start(
-                    out=x_raw[(a, c)][:].rearrange("p (j e) -> p j e", e=E),
-                    in_=view[:, j0:j1, :],
+                    out=chunk[:].rearrange("p (j e) -> p j e", e=E), in_=view[:, j0:j1, :]
                 )
-            for j in range(j0, j1):
-                where[j] = (c, j - j0)
-            if c == 0:
-                nc.sync.dma_start(out=w1_raw[:], in_=W1.rearrange("h (p j) m -> (h p) (j m)", j=4))
-            if c == 2:
-                nc.sync.dma_start(
-                    out=bias[:], in_=b1.rearrange("h m -> (h m)").partition_broadcast(P)
-                )
+                for j in range(j0, j1):
+                    x_raw[(a, j)] = chunk[:, (j - j0) * E : (j - j0 + 1) * E]
+
+        w1_raw = const.tile([P, 4 * M], BF16, name="w1_raw")
+        bias = const.tile([P, M], BF16, name="bias")
+        load_w("q", Wq)
+        load_w("k", Wk)
+        load_x(0, 2)
+        load_w("v", Wv)
+        load_x(2, 4)
+        load_x(4, 8)
+        nc.sync.dma_start(out=w1_raw[:], in_=W1.rearrange("h (p j) m -> (h p) (j m)", j=4))
+        load_x(8, 12)
+        nc.sync.dma_start(out=bias[:], in_=b1.rearrange("h m -> (h m)").partition_broadcast(P))
+        for j in range(12, TILES, 4):
+            load_x(j, j + 4)
 
         ident = const.tile([P, P], F32, name="ident")
         make_identity(nc, ident[:])
@@ -87,23 +87,20 @@ def tile_treehopnode_pa_t_kernel(tc, q, rep, Wq, Wk, Wv, W1, b1, out):
         w1_code = const.tile([P, M], U32, name="w1_code", align_bytes=64)
         w1_scale = const.tile([P, M], U8, name="w1_scale", align_bytes=64)
 
-        def regroup_w(key):
+        def regroup_w(key, on_vector, on_scalar):
             src = w_raw[key][:].rearrange("p (j c t) -> p c j t", j=4, t=4)
             dst = w_grp[key][:].rearrange("p (t c j) -> p c j t", t=4, j=4)
-            nc.vector.tensor_copy(out=dst[:, 0:64], in_=src[:, 0:64])
-            nc.scalar.copy(out=dst[:, 64:128], in_=src[:, 64:128])
+            v0, v1 = on_vector
+            s0, s1 = on_scalar
+            if v1 > v0:
+                nc.vector.tensor_copy(out=dst[:, v0:v1], in_=src[:, v0:v1])
+            if s1 > s0:
+                nc.scalar.copy(out=dst[:, s0:s1], in_=src[:, s0:s1])
 
         def quantise_w(key):
             nc.vector.quantize_mx(
                 out=w_code[key][:].bitcast(FP8X4), scales=w_scale[key][:], in_=w_grp[key][:]
             )
-
-        regroup_w("q")
-        regroup_w("k")
-        quantise_w("q")
-        regroup_w("v")
-        quantise_w("k")
-        quantise_w("v")
 
         tb = {}
         grp = {}
@@ -118,19 +115,18 @@ def tile_treehopnode_pa_t_kernel(tc, q, rep, Wq, Wk, Wv, W1, b1, out):
         z_scale = {}
         o_bank = {}
         o_sb = {}
+        o_last = {}
 
         def transposes(r):
             for j in (2 * r, 2 * r + 1):
-                c, jj = where[j]
                 tb[j] = tb_pool.tile([P, 512], F32, name="tb")
                 for a in range(2):
-                    words = x_raw[(a, c)][:].bitcast(F32)
+                    words = x_raw[(a, j)].bitcast(F32)
                     for u in range(2):
                         s = 2 * a + u
-                        w0 = jj * (E // 2) + u
                         nc.tensor.transpose(
                             out=tb[j][:, s * P : (s + 1) * P],
-                            in_=words[:, w0 : w0 + 2 * P - 1 : 2],
+                            in_=words[:, u : u + 2 * P - 1 : 2],
                             identity=ident[:],
                         )
 
@@ -197,11 +193,45 @@ def tile_treehopnode_pa_t_kernel(tc, q, rep, Wq, Wk, Wv, W1, b1, out):
             if i == 0:
                 z_grp[r] = z_pool.tile([P, 1024], BF16, name="z_grp", align_bytes=64)
             nc.vector.tensor_tensor(
-                out=z_grp[r][:, i * 512 : (i + 1) * 512].rearrange("p (c i t) -> p c t i", i=2, t=4),
-                in0=gate[j][:].rearrange("p (t c i) -> p c t i", t=4, i=2),
-                in1=banks[("v", j)][:].rearrange("p (t c i) -> p c t i", t=4, i=2),
+                out=z_grp[r][:, i * 512 : (i + 1) * 512].rearrange("p (c i t) -> p c t i", i=4, t=4),
+                in0=gate[j][:].rearrange("p (t c i) -> p c t i", t=4, i=4),
+                in1=banks[("v", j)][:].rearrange("p (t c i) -> p c t i", t=4, i=4),
                 op=ALU.mult,
             )
+
+        def quantise_z_tile(j):
+            r, i = divmod(j, 2)
+            if i == 0:
+                z_code[r] = z_pool.tile([P, 256], U32, name="z_code", align_bytes=64)
+                z_scale[r] = z_pool.tile([P, 256], U8, name="z_scale", align_bytes=64)
+            nc.vector.quantize_mx(
+                out=z_code[r][:, i * P : (i + 1) * P].bitcast(FP8X4),
+                scales=z_scale[r][:, i * P : (i + 1) * P],
+                in_=z_grp[r][:, i * 512 : (i + 1) * 512],
+            )
+
+        def layer_tile(j, bank):
+            r, i = divmod(j, 2)
+            o_bank[j] = bank
+            nc.tensor.matmul_mx(
+                out=bank[:, 0:M],
+                lhsT=z_code[r][:, i * P : (i + 1) * P].bitcast(FP8X4),
+                lhsT_scale=z_scale[r][:, i * P : (i + 1) * P],
+                rhs=w1_code[:].bitcast(FP8X4),
+                rhs_scale=w1_scale[:],
+                start=True,
+                stop=True,
+            )
+
+        def finish_tile(j):
+            o_last[j] = o_pool.tile([P, M], F32, name="o_last")
+            nc.vector.tensor_tensor(
+                out=o_last[j][:], in0=o_bank[j][:, 0:M], in1=bias[:], op=ALU.add
+            )
+
+        def relu_store_tile(j):
+            nc.scalar.activation(out=o_last[j][:], in_=o_last[j][:], func=ACT.Relu)
+            nc.sync.dma_start(out=out_view[:, j, :], in_=o_last[j][:])
 
         def quantise_z(r):
             z_code[r] = z_pool.tile([P, 256], U32, name="z_code", align_bytes=64)
@@ -242,7 +272,40 @@ def tile_treehopnode_pa_t_kernel(tc, q, rep, Wq, Wk, Wv, W1, b1, out):
         def ok(r):
             return 0 <= r < PAIRS
 
-        for r in range(-3, PAIRS + 2):
+        def regroup_w1():
+            nc.vector.tensor_copy(
+                out=w1_grp[:].rearrange("p (m j) -> p m j", j=4),
+                in_=w1_raw[:].rearrange("p (j m) -> p m j", j=4),
+            )
+
+        def quantise_w1():
+            nc.vector.quantize_mx(
+                out=w1_code[:].bitcast(FP8X4), scales=w1_scale[:], in_=w1_grp[:]
+            )
+
+        regroup_w("q", (0, 64), (64, 128))
+        transposes(0)
+        regroup_w("k", (0, 64), (64, 128))
+        quantise_w("q")
+        evacuate(0)
+        evacuate(1)
+        quantise_w("k")
+        regroup_w("v", (0, 64), (0, 0))
+        transposes(1)
+        quantise_x(0)
+        project("q", 0)
+        project("q", 1)
+        project("k", 0)
+        project("k", 1)
+        evacuate(2)
+        evacuate(3)
+        copy_q(0)
+        regroup_w("v", (64, 128), (0, 0))
+        quantise_w("v")
+        quantise_x(1)
+        transposes(2)
+
+        for r in range(PAIRS):
             if ok(r - 2):
                 layer(r - 2)
             if ok(r):
@@ -252,7 +315,8 @@ def tile_treehopnode_pa_t_kernel(tc, q, rep, Wq, Wk, Wv, W1, b1, out):
             if ok(r - 1):
                 gated(2 * r - 1)
             if ok(r):
-                project("k", 2 * r + 1)
+                if r > 0:
+                    project("k", 2 * r + 1)
             if ok(r + 1):
                 project("q", 2 * r + 2)
             if ok(r - 2):
@@ -279,16 +343,25 @@ def tile_treehopnode_pa_t_kernel(tc, q, rep, Wq, Wk, Wv, W1, b1, out):
                 copy_q(2 * r + 2)
             if ok(r - 2):
                 relu_store(r - 2)
+            if r == 0:
+                regroup_w1()
+            if r == 1:
+                quantise_w1()
             if ok(r - 1):
                 quantise_z(r - 1)
             if ok(r + 2):
                 quantise_x(r + 2)
-            if r == -2:
-                nc.vector.tensor_copy(
-                    out=w1_grp[:].rearrange("p (m j) -> p m j", j=4),
-                    in_=w1_raw[:].rearrange("p (j m) -> p m j", j=4),
-                )
-            if r == -1:
-                nc.vector.quantize_mx(
-                    out=w1_code[:].bitcast(FP8X4), scales=w1_scale[:], in_=w1_grp[:]
-                )
+
+        a, b = TILES - 2, TILES - 1
+        quantise_z_tile(a)
+        layer(PAIRS - 2)
+        gated(b)
+        layer_tile(a, qb_pool.tile([P, 512], F32, name="bank_q"))
+        quantise_z_tile(b)
+        finish(PAIRS - 2)
+        relu_store(PAIRS - 2)
+        layer_tile(b, kb_pool.tile([P, 512], F32, name="bank_k"))
+        finish_tile(a)
+        relu_store_tile(a)
+        finish_tile(b)
+        relu_store_tile(b)

@@ -330,23 +330,24 @@ def tile_treehopnode_pa_t_kernel(tc, q, rep, Wq, Wk, Wv, W1, b1, out):
                 project("q", 2 * r + 3)
             if ok(r):
                 product(2 * r + 1)
+            if ok(r + 1):
+                copy_q(2 * r + 2)
+            if ok(r):
                 sigmoid(2 * r + 1)
             if ok(r + 1):
                 project("k", 2 * r + 2)
             if ok(r):
+                if r == 0:
+                    regroup_w1()
+                if r == 1:
+                    quantise_w1()
                 gated(2 * r)
             if ok(r + 3):
                 transposes(r + 3)
             if ok(r):
                 project("v", 2 * r + 1)
-            if ok(r + 1):
-                copy_q(2 * r + 2)
             if ok(r - 2):
                 relu_store(r - 2)
-            if r == 0:
-                regroup_w1()
-            if r == 1:
-                quantise_w1()
             if ok(r - 1):
                 quantise_z(r - 1)
             if ok(r + 2):

@@ -75,6 +75,15 @@ def tile_treehopnode_pa_t_kernel(tc, q, rep, Wq, Wk, Wv, W1, b1, out):
         warm_out = const.tile([P, 1], F32, name="warm_out")
         nc.vector.memset(warm_in[:], 0.0)
         nc.scalar.activation(out=warm_out[:], in_=warm_in[:], func=ACT.Sigmoid)
+        zeros = const.tile([P, 512], BF16, name="zeros")
+        nc.vector.memset(zeros[:], 0.0)
+
+        def keep_warm(count):
+            bank = ob_pool.tile([P, 512], F32, name="o_bank")
+            for dummy in range(count):
+                nc.tensor.matmul(
+                    out=bank[:], lhsT=zeros[:, 0:P], rhs=zeros[:], start=True, stop=True
+                )
 
         w_grp = {}
         w_code = {}
@@ -148,11 +157,11 @@ def tile_treehopnode_pa_t_kernel(tc, q, rep, Wq, Wk, Wv, W1, b1, out):
                 out=x_code[r][:].bitcast(FP8X4), scales=x_scale[r][:], in_=grp[r][:]
             )
 
-        def project(key, j):
+        def project(key, j, spare=None):
             r, i = divmod(j, 2)
             a = 0 if key == "q" else 1
             pool = {"q": qb_pool, "k": kb_pool, "v": vb_pool}[key]
-            bank = pool.tile([P, 512], F32, name="bank_" + key)
+            bank = pool.tile([P, 512], F32, name="bank_" + key) if spare is None else spare
             banks[(key, j)] = bank
             c0 = (2 * i + a) * P
             for t in range(4):
@@ -284,7 +293,9 @@ def tile_treehopnode_pa_t_kernel(tc, q, rep, Wq, Wk, Wv, W1, b1, out):
             )
 
         regroup_w("q", (0, 64), (64, 128))
+        keep_warm(12)
         transposes(0)
+        keep_warm(2)
         regroup_w("k", (0, 64), (64, 128))
         quantise_w("q")
         evacuate(0)
@@ -305,7 +316,7 @@ def tile_treehopnode_pa_t_kernel(tc, q, rep, Wq, Wk, Wv, W1, b1, out):
         quantise_x(1)
         transposes(2)
 
-        for r in range(PAIRS):
+        for r in range(PAIRS - 1):
             if ok(r - 2):
                 layer(r - 2)
             if ok(r):
@@ -353,16 +364,34 @@ def tile_treehopnode_pa_t_kernel(tc, q, rep, Wq, Wk, Wv, W1, b1, out):
             if ok(r + 2):
                 quantise_x(r + 2)
 
+        last = PAIRS - 1
         a, b = TILES - 2, TILES - 1
+        layer(last - 2)
+        copy_q(b)
+        product(a)
+        project("k", b)
+        sigmoid(a)
+        gated(a - 1)
+        project("v", a)
+        finish(last - 2)
+        product(b)
+        sigmoid(b)
+        relu_store(last - 2)
+        quantise_z(last - 1)
+        layer(last - 1)
+        project("v", b, tb_pool.tile([P, 512], F32, name="tb"))
+        gated(a)
         quantise_z_tile(a)
-        layer(PAIRS - 2)
-        gated(b)
+        finish(last - 1)
+        relu_store(last - 1)
         layer_tile(a, qb_pool.tile([P, 512], F32, name="bank_q"))
+        gated(b)
         quantise_z_tile(b)
-        finish(PAIRS - 2)
-        relu_store(PAIRS - 2)
-        layer_tile(b, kb_pool.tile([P, 512], F32, name="bank_k"))
         finish_tile(a)
         relu_store_tile(a)
+        layer_tile(b, kb_pool.tile([P, 512], F32, name="bank_k"))
         finish_tile(b)
-        relu_store_tile(b)
+        nc.vector.tensor_scalar(
+            out=o_last[b][:], in0=o_last[b][:], scalar1=0.0, scalar2=None, op0=ALU.max
+        )
+        nc.sync.dma_start(out=out_view[:, b, :], in_=o_last[b][:])

@@ -322,6 +322,9 @@ def tile_treehopnode_pa_t_kernel(tc, q, rep, Wq, Wk, Wv, W1, b1, out):
             if ok(r):
                 copy_q(2 * r + 1)
                 product(2 * r)
+            if ok(r + 2):
+                evacuate(2 * r + 4)
+            if ok(r):
                 sigmoid(2 * r)
             if ok(r - 1):
                 gated(2 * r - 1)
@@ -333,29 +336,26 @@ def tile_treehopnode_pa_t_kernel(tc, q, rep, Wq, Wk, Wv, W1, b1, out):
             if ok(r - 2):
                 finish(r - 2)
             if ok(r):
-                project("v", 2 * r)
-            if ok(r + 2):
-                evacuate(2 * r + 4)
-                evacuate(2 * r + 5)
-            if ok(r + 1):
-                project("q", 2 * r + 3)
-            if ok(r):
                 product(2 * r + 1)
+            if ok(r + 2):
+                evacuate(2 * r + 5)
             if ok(r + 1):
                 copy_q(2 * r + 2)
             if ok(r):
                 sigmoid(2 * r + 1)
             if ok(r + 1):
                 project("k", 2 * r + 2)
+                project("q", 2 * r + 3)
             if ok(r):
-                if r == 0:
-                    regroup_w1()
-                if r == 1:
-                    quantise_w1()
-                gated(2 * r)
+                project("v", 2 * r)
+            if r == 0:
+                regroup_w1()
+            if r == 1:
+                quantise_w1()
             if ok(r + 3):
                 transposes(r + 3)
             if ok(r):
+                gated(2 * r)
                 project("v", 2 * r + 1)
             if ok(r - 2):
                 relu_store(r - 2)

@@ -57,11 +57,11 @@ def tile_treehopnode_pa_t_kernel(tc, q, rep, Wq, Wk, Wv, W1, b1, out):
 
         w1_raw = const.tile([P, 4 * M], BF16, name="w1_raw")
         bias = const.tile([P, M], BF16, name="bias")
+        load_x(0, 2)
         load_w("q", Wq)
         load_w("k", Wk)
-        load_x(0, 2)
-        load_w("v", Wv)
         load_x(2, 4)
+        load_w("v", Wv)
         load_x(4, 8)
         nc.sync.dma_start(out=w1_raw[:], in_=W1.rearrange("h (p j) m -> (h p) (j m)", j=4))
         load_x(8, 12)
@@ -272,7 +272,17 @@ def tile_treehopnode_pa_t_kernel(tc, q, rep, Wq, Wk, Wv, W1, b1, out):
             )
 
         def relu_store(r):
-            nc.scalar.activation(out=o_sb[r][:], in_=o_sb[r][:], func=ACT.Relu)
+            if r < PAIRS - 3:
+                nc.gpsimd.tensor_scalar(
+                    out=o_sb[r][:],
+                    in0=o_sb[r][:],
+                    scalar1=0.0,
+                    scalar2=0.0,
+                    op0=ALU.max,
+                    op1=ALU.add,
+                )
+            else:
+                nc.scalar.activation(out=o_sb[r][:], in_=o_sb[r][:], func=ACT.Relu)
             nc.sync.dma_start(
                 out=out_view[:, 2 * r : 2 * r + 2, :],
                 in_=o_sb[r][:].rearrange("p (j m) -> p j m", m=M),
@@ -292,27 +302,26 @@ def tile_treehopnode_pa_t_kernel(tc, q, rep, Wq, Wk, Wv, W1, b1, out):
                 out=w1_code[:].bitcast(FP8X4), scales=w1_scale[:], in_=w1_grp[:]
             )
 
-        regroup_w("q", (0, 64), (64, 128))
-        keep_warm(12)
+        keep_warm(6)
         transposes(0)
         keep_warm(2)
-        regroup_w("k", (0, 64), (64, 128))
-        quantise_w("q")
         evacuate(0)
         evacuate(1)
-        quantise_w("k")
-        regroup_w("v", (0, 64), (0, 0))
-        transposes(1)
+        regroup_w("q", (0, 96), (96, 128))
         quantise_x(0)
+        regroup_w("k", (0, 64), (64, 128))
+        transposes(1)
+        quantise_w("q")
         project("q", 0)
         project("q", 1)
-        project("k", 0)
-        project("k", 1)
+        quantise_w("k")
         evacuate(2)
         evacuate(3)
+        project("k", 0)
+        project("k", 1)
         copy_q(0)
-        regroup_w("v", (64, 128), (0, 0))
-        quantise_w("v")
+        copy_q(1)
+        regroup_w("v", (0, 96), (96, 128))
         quantise_x(1)
         transposes(2)
 
@@ -320,7 +329,8 @@ def tile_treehopnode_pa_t_kernel(tc, q, rep, Wq, Wk, Wv, W1, b1, out):
             if ok(r - 2):
                 layer(r - 2)
             if ok(r):
-                copy_q(2 * r + 1)
+                if r > 0:
+                    copy_q(2 * r + 1)
                 product(2 * r)
             if ok(r + 2):
                 evacuate(2 * r + 4)
@@ -347,6 +357,8 @@ def tile_treehopnode_pa_t_kernel(tc, q, rep, Wq, Wk, Wv, W1, b1, out):
                 project("k", 2 * r + 2)
                 project("q", 2 * r + 3)
             if ok(r):
+                if r == 0:
+                    quantise_w("v")
                 project("v", 2 * r)
             if r == 0:
                 regroup_w1()

@@ -176,10 +176,10 @@ def tile_treehopnode_pa_t_kernel(tc, q, rep, Wq, Wk, Wv, W1, b1, out):
                 )
 
         def by_node(ap):
-            return ap
+            return ap.rearrange("p (t n) -> p n t", t=4)
 
         def flat(ap):
-            return ap
+            return ap.rearrange("p (n t) -> p n t", t=4)
 
         def copy_q(j):
             q_sb[j] = f32_pool.tile([P, 512], F32, name="q_sb")
@@ -202,9 +202,9 @@ def tile_treehopnode_pa_t_kernel(tc, q, rep, Wq, Wk, Wv, W1, b1, out):
             if i == 0:
                 z_grp[r] = z_pool.tile([P, 1024], BF16, name="z_grp", align_bytes=64)
             nc.vector.tensor_tensor(
-                out=z_grp[r][:, i * 512 : (i + 1) * 512].rearrange("p (c i t) -> p c t i", i=4, t=4),
-                in0=gate[j][:].rearrange("p (t c i) -> p c t i", t=4, i=4),
-                in1=banks[("v", j)][:].rearrange("p (t c i) -> p c t i", t=4, i=4),
+                out=flat(z_grp[r][:, i * 512 : (i + 1) * 512]),
+                in0=flat(gate[j][:]),
+                in1=by_node(banks[("v", j)][:]),
                 op=ALU.mult,
             )
 

import math
from contextlib import ExitStack

import concourse.mybir as mybir
from concourse.masks import make_identity

F32 = mybir.dt.float32
BF16 = mybir.dt.bfloat16
U32 = mybir.dt.uint32
U8 = mybir.dt.uint8
FP8X4 = mybir.dt.float8_e4m3fn_x4
ALU = mybir.AluOpType
ACT = mybir.ActivationFunctionType

P = 128
NODES, E, G, M = 4096, 512, 512, 256
TILES = NODES // P
PAIRS = TILES // 2
FLOPS = 2 * NODES * E * 3 * G + 2 * NODES * G * M


def tile_treehopnode_pa_t_kernel(tc, q, rep, Wq, Wk, Wv, W1, b1, out):
    nc = tc.nc
    q_view = q.rearrange("(p j) e -> p j e", j=TILES)
    rep_view = rep.rearrange("(p j) e -> p j e", j=TILES)
    out_view = out.rearrange("(p j) h m -> p j (h m)", j=TILES)

    with ExitStack() as ctx:
        const = ctx.enter_context(tc.tile_pool(name="const", bufs=1))
        grp_pool = ctx.enter_context(tc.tile_pool(name="grp_pool", bufs=3))
        code_pool = ctx.enter_context(tc.tile_pool(name="code_pool", bufs=4))
        f32_pool = ctx.enter_context(tc.tile_pool(name="f32_pool", bufs=3))
        z_pool = ctx.enter_context(tc.tile_pool(name="z_pool", bufs=3))
        o_pool = ctx.enter_context(tc.tile_pool(name="o_pool", bufs=4))
        tb_pool = ctx.enter_context(tc.psum_pool(name="tb_pool", bufs=2))
        qb_pool = ctx.enter_context(tc.psum_pool(name="qb_pool", bufs=2))
        kb_pool = ctx.enter_context(tc.psum_pool(name="kb_pool", bufs=2))
        vb_pool = ctx.enter_context(tc.psum_pool(name="vb_pool", bufs=1))
        ob_pool = ctx.enter_context(tc.psum_pool(name="ob_pool", bufs=1))
        ctx.enter_context(tc.manual_schedule())

        w_raw = {}
        x_raw = {}

        def load_w(key, w):
            w_raw[key] = const.tile([P, 4 * G], BF16, name="w_raw_" + key)
            nc.sync.dma_start(out=w_raw[key][:], in_=w.rearrange("(p j) g -> p (j g)", j=4))

        def load_x(j0, j1):
            for a, view in enumerate((q_view, rep_view)):
                chunk = const.tile([P, (j1 - j0) * E], BF16, name="x_raw_%d_%d" % (a, j0))
                nc.sync.dma_start(
                    out=chunk[:].rearrange("p (j e) -> p j e", e=E), in_=view[:, j0:j1, :]
                )
                for j in range(j0, j1):
                    x_raw[(a, j)] = chunk[:, (j - j0) * E : (j - j0 + 1) * E]

        w1_raw = const.tile([P, 4 * M], BF16, name="w1_raw")
        bias = const.tile([P, M], BF16, name="bias")
        load_x(0, 2)
        load_w("q", Wq)
        load_w("k", Wk)
        load_x(2, 4)
        load_w("v", Wv)
        load_x(4, 8)
        nc.sync.dma_start(out=w1_raw[:], in_=W1.rearrange("h (p j) m -> (h p) (j m)", j=4))
        load_x(8, 12)
        nc.sync.dma_start(out=bias[:], in_=b1.rearrange("h m -> (h m)").partition_broadcast(P))
        for j in range(12, TILES, 4):
            load_x(j, j + 4)

        ident = const.tile([P, P], F32, name="ident")
        make_identity(nc, ident[:])
        warm_in = const.tile([P, 1], F32, name="warm_in")
        warm_out = const.tile([P, 1], F32, name="warm_out")
        nc.vector.memset(warm_in[:], 0.0)
        nc.scalar.activation(out=warm_out[:], in_=warm_in[:], func=ACT.Sigmoid)
        zeros = const.tile([P, 512], BF16, name="zeros")
        nc.vector.memset(zeros[:], 0.0)

        def keep_warm(count):
            bank = ob_pool.tile([P, 512], F32, name="o_bank")
            for dummy in range(count):
                nc.tensor.matmul(
                    out=bank[:], lhsT=zeros[:, 0:P], rhs=zeros[:], start=True, stop=True
                )

        w_grp = {}
        w_code = {}
        w_scale = {}
        for key in ("q", "k", "v"):
            w_grp[key] = const.tile([P, 4 * G], BF16, name="w_grp_" + key, align_bytes=64)
            w_code[key] = const.tile([P, G], U32, name="w_code_" + key, align_bytes=64)
            w_scale[key] = const.tile([P, G], U8, name="w_scale_" + key, align_bytes=64)
        w1_grp = const.tile([P, 4 * M], BF16, name="w1_grp", align_bytes=64)
        w1_code = const.tile([P, M], U32, name="w1_code", align_bytes=64)
        w1_scale = const.tile([P, M], U8, name="w1_scale", align_bytes=64)

        def regroup_w(key, on_vector, on_scalar):
            src = w_raw[key][:].rearrange("p (j c t) -> p c j t", j=4, t=4)
            dst = w_grp[key][:].rearrange("p (t c j) -> p c j t", t=4, j=4)
            v0, v1 = on_vector
            s0, s1 = on_scalar
            if v1 > v0:
                nc.vector.tensor_copy(out=dst[:, v0:v1], in_=src[:, v0:v1])
            if s1 > s0:
                nc.scalar.copy(out=dst[:, s0:s1], in_=src[:, s0:s1])

        def quantise_w(key):
            nc.vector.quantize_mx(
                out=w_code[key][:].bitcast(FP8X4), scales=w_scale[key][:], in_=w_grp[key][:]
            )

        tb = {}
        grp = {}
        x_code = {}
        x_scale = {}
        banks = {}
        q_sb = {}
        prod = {}
        gate = {}
        z_grp = {}
        z_code = {}
        z_scale = {}
        o_bank = {}
        o_sb = {}
        o_last = {}

        def transposes(r):
            for j in (2 * r, 2 * r + 1):
                tb[j] = tb_pool.tile([P, 512], F32, name="tb")
                for a in range(2):
                    words = x_raw[(a, j)].bitcast(F32)
                    for u in range(2):
                        s = 2 * a + u
                        nc.tensor.transpose(
                            out=tb[j][:, s * P : (s + 1) * P],
                            in_=words[:, u : u + 2 * P - 1 : 2],
                            identity=ident[:],
                        )

        def evacuate(j):
            r, i = divmod(j, 2)
            if i == 0:
                grp[r] = grp_pool.tile([P, 2048], BF16, name="grp", align_bytes=64)
            nc.scalar.copy(
                out=grp[r][:, i * 1024 : (i + 1) * 1024]
                .bitcast(F32)
                .rearrange("p (a n u) -> p a n u", a=2, u=2),
                in_=tb[j][:].rearrange("p (a u n) -> p a n u", a=2, u=2),
            )

        def quantise_x(r):
            x_code[r] = code_pool.tile([P, 512], U32, name="x_code", align_bytes=64)
            x_scale[r] = code_pool.tile([P, 512], U8, name="x_scale", align_bytes=64)
            nc.vector.quantize_mx(
                out=x_code[r][:].bitcast(FP8X4), scales=x_scale[r][:], in_=grp[r][:]
            )

        def project(key, j, spare=None):
            r, i = divmod(j, 2)
            a = 0 if key == "q" else 1
            pool = {"q": qb_pool, "k": kb_pool, "v": vb_pool}[key]
            bank = pool.tile([P, 512], F32, name="bank_" + key) if spare is None else spare
            banks[(key, j)] = bank
            c0 = (2 * i + a) * P
            for t in range(4):
                nc.tensor.matmul_mx(
                    out=bank[:, t * P : (t + 1) * P],
                    lhsT=w_code[key][:, t * P : (t + 1) * P].bitcast(FP8X4),
                    lhsT_scale=w_scale[key][:, t * P : (t + 1) * P],
                    rhs=x_code[r][:, c0 : c0 + P].bitcast(FP8X4),
                    rhs_scale=x_scale[r][:, c0 : c0 + P],
                    start=True,
                    stop=True,
                )

        def by_node(ap):
            return ap.rearrange("p (t n) -> p n t", t=4)

        def flat(ap):
            return ap.rearrange("p (n t) -> p n t", t=4)

        def copy_q(j):
            q_sb[j] = f32_pool.tile([P, 512], F32, name="q_sb")
            nc.scalar.copy(out=flat(q_sb[j][:]), in_=by_node(banks[("q", j)][:]))

        def product(j):
            prod[j] = f32_pool.tile([P, 512], F32, name="prod")
            nc.vector.tensor_tensor(
                out=flat(prod[j][:]), in0=flat(q_sb[j][:]), in1=by_node(banks[("k", j)][:]), op=ALU.mult
            )

        def sigmoid(j):
            gate[j] = f32_pool.tile([P, 512], F32, name="gate")
            nc.scalar.activation(
                out=gate[j][:], in_=prod[j][:], func=ACT.Sigmoid, scale=1.0 / math.sqrt(G)
            )

        def gated(j):
            r, i = divmod(j, 2)
            if i == 0:
                z_grp[r] = z_pool.tile([P, 1024], BF16, name="z_grp", align_bytes=64)
            nc.vector.tensor_tensor(
                out=flat(z_grp[r][:, i * 512 : (i + 1) * 512]),
                in0=flat(gate[j][:]),
                in1=by_node(banks[("v", j)][:]),
                op=ALU.mult,
            )

        def quantise_z_tile(j):
            r, i = divmod(j, 2)
            if i == 0:
                z_code[r] = z_pool.tile([P, 256], U32, name="z_code", align_bytes=64)
                z_scale[r] = z_pool.tile([P, 256], U8, name="z_scale", align_bytes=64)
            nc.vector.quantize_mx(
                out=z_code[r][:, i * P : (i + 1) * P].bitcast(FP8X4),
                scales=z_scale[r][:, i * P : (i + 1) * P],
                in_=z_grp[r][:, i * 512 : (i + 1) * 512],
            )

        def layer_tile(j, bank):
            r, i = divmod(j, 2)
            o_bank[j] = bank
            nc.tensor.matmul_mx(
                out=bank[:, 0:M],
                lhsT=z_code[r][:, i * P : (i + 1) * P].bitcast(FP8X4),
                lhsT_scale=z_scale[r][:, i * P : (i + 1) * P],
                rhs=w1_code[:].bitcast(FP8X4),
                rhs_scale=w1_scale[:],
                start=True,
                stop=True,
            )

        def finish_tile(j):
            o_last[j] = o_pool.tile([P, M], F32, name="o_last")
            nc.vector.tensor_tensor(
                out=o_last[j][:], in0=o_bank[j][:, 0:M], in1=bias[:], op=ALU.add
            )

        def relu_store_tile(j):
            nc.scalar.activation(out=o_last[j][:], in_=o_last[j][:], func=ACT.Relu)
            nc.sync.dma_start(out=out_view[:, j, :], in_=o_last[j][:])

        def quantise_z(r):
            z_code[r] = z_pool.tile([P, 256], U32, name="z_code", align_bytes=64)
            z_scale[r] = z_pool.tile([P, 256], U8, name="z_scale", align_bytes=64)
            nc.vector.quantize_mx(
                out=z_code[r][:].bitcast(FP8X4), scales=z_scale[r][:], in_=z_grp[r][:]
            )

        def layer(r):
            o_bank[r] = ob_pool.tile([P, 512], F32, name="o_bank")
            for i in range(2):
                nc.tensor.matmul_mx(
                    out=o_bank[r][:, i * M : (i + 1) * M],
                    lhsT=z_code[r][:, i * P : (i + 1) * P].bitcast(FP8X4),
                    lhsT_scale=z_scale[r][:, i * P : (i + 1) * P],
                    rhs=w1_code[:].bitcast(FP8X4),
                    rhs_scale=w1_scale[:],
                    start=True,
                    stop=True,
                )

        def finish(r):
            o_sb[r] = o_pool.tile([P, 512], F32, name="o_sb")
            nc.vector.tensor_tensor(
                out=o_sb[r][:].rearrange("p (i m) -> p i m", i=2),
                in0=o_bank[r][:].rearrange("p (i m) -> p i m", i=2),
                in1=bias[:].unsqueeze(1).to_broadcast([P, 2, M]),
                op=ALU.add,
            )

        def relu_store(r):
            if r < PAIRS - 3:
                nc.gpsimd.tensor_scalar(
                    out=o_sb[r][:],
                    in0=o_sb[r][:],
                    scalar1=0.0,
                    scalar2=0.0,
                    op0=ALU.max,
                    op1=ALU.add,
                )
            else:
                nc.scalar.activation(out=o_sb[r][:], in_=o_sb[r][:], func=ACT.Relu)
            nc.sync.dma_start(
                out=out_view[:, 2 * r : 2 * r + 2, :],
                in_=o_sb[r][:].rearrange("p (j m) -> p j m", m=M),
            )

        def ok(r):
            return 0 <= r < PAIRS

        def regroup_w1():
            nc.vector.tensor_copy(
                out=w1_grp[:].rearrange("p (m j) -> p m j", j=4),
                in_=w1_raw[:].rearrange("p (j m) -> p m j", j=4),
            )

        def quantise_w1():
            nc.vector.quantize_mx(
                out=w1_code[:].bitcast(FP8X4), scales=w1_scale[:], in_=w1_grp[:]
            )

        keep_warm(6)
        transposes(0)
        keep_warm(2)
        evacuate(0)
        evacuate(1)
        regroup_w("q", (0, 96), (96, 128))
        quantise_x(0)
        regroup_w("k", (0, 64), (64, 128))
        transposes(1)
        quantise_w("q")
        project("q", 0)
        project("q", 1)
        quantise_w("k")
        evacuate(2)
        evacuate(3)
        project("k", 0)
        project("k", 1)
        copy_q(0)
        copy_q(1)
        regroup_w("v", (0, 96), (96, 128))
        quantise_x(1)
        transposes(2)

        for r in range(PAIRS - 1):
            if ok(r - 2):
                layer(r - 2)
            if ok(r):
                if r > 0:
                    copy_q(2 * r + 1)
                product(2 * r)
            if ok(r + 2):
                evacuate(2 * r + 4)
            if ok(r):
                sigmoid(2 * r)
            if ok(r - 1):
                gated(2 * r - 1)
            if ok(r):
                if r > 0:
                    project("k", 2 * r + 1)
            if ok(r + 1):
                project("q", 2 * r + 2)
            if ok(r - 2):
                finish(r - 2)
            if ok(r):
                product(2 * r + 1)
            if ok(r + 2):
                evacuate(2 * r + 5)
            if ok(r + 1):
                copy_q(2 * r + 2)
            if ok(r):
                sigmoid(2 * r + 1)
            if ok(r + 1):
                project("k", 2 * r + 2)
                project("q", 2 * r + 3)
            if ok(r):
                if r == 0:
                    quantise_w("v")
                project("v", 2 * r)
            if r == 0:
                regroup_w1()
            if r == 1:
                quantise_w1()
            if ok(r + 3):
                transposes(r + 3)
            if ok(r):
                gated(2 * r)
                project("v", 2 * r + 1)
            if ok(r - 2):
                relu_store(r - 2)
            if ok(r - 1):
                quantise_z(r - 1)
            if ok(r + 2):
                quantise_x(r + 2)

        last = PAIRS - 1
        a, b = TILES - 2, TILES - 1
        layer(last - 2)
        copy_q(b)
        product(a)
        project("k", b)
        sigmoid(a)
        gated(a - 1)
        project("v", a)
        finish(last - 2)
        product(b)
        sigmoid(b)
        relu_store(last - 2)
        quantise_z(last - 1)
        layer(last - 1)
        project("v", b, tb_pool.tile([P, 512], F32, name="tb"))
        gated(a)
        quantise_z_tile(a)
        finish(last - 1)
        relu_store(last - 1)
        layer_tile(a, qb_pool.tile([P, 512], F32, name="bank_q"))
        gated(b)
        quantise_z_tile(b)
        finish_tile(a)
        relu_store_tile(a)
        layer_tile(b, kb_pool.tile([P, 512], F32, name="bank_k"))
        finish_tile(b)
        nc.vector.tensor_scalar(
            out=o_last[b][:], in0=o_last[b][:], scalar1=0.0, scalar2=None, op0=ALU.max
        )
        nc.sync.dma_start(out=out_view[:, b, :], in_=o_last[b][:])
